import numpy as np
import ml_dtypes


def mxq(x, axis, fmt="e4m3"):
    dtype, down = {"e4m3": (ml_dtypes.float8_e4m3fn, 7), "e5m2": (ml_dtypes.float8_e5m2, 14)}[fmt]
    v = np.moveaxis(np.asarray(x, np.float32).astype(ml_dtypes.bfloat16).astype(np.float64), axis, -1)
    blocks = v.reshape(v.shape[:-1] + (-1, 32))
    amax = np.abs(blocks).max(-1, keepdims=True)
    byte = np.maximum(np.where(amax > 0, np.frexp(amax)[1] - 1 + 127, 0) - down, 1)
    scale = np.exp2(byte - 127.0)
    codes = (blocks / scale).astype(np.float32).astype(dtype).astype(np.float64)
    return np.moveaxis((codes * scale).reshape(v.shape), -1, axis)


WIDE = False


def mx_kscale(k):
    if not WIDE:
        return np.ones(k)
    levels = np.array([30, -30])
    if k % 512:
        return np.exp2(np.random.permutation(np.resize(levels, k // 32))).repeat(32)
    a = np.empty((k // 512, 16))
    for p in range(k // 512):
        a[p, :8] = np.random.permutation(np.resize(levels, 8))
        for g in range(8):
            far = levels[np.abs(levels - a[p, g]) >= 10]
            a[p, g + 8] = far[np.random.randint(len(far))]
    return np.exp2(a.ravel()).repeat(32)


BF16 = ml_dtypes.bfloat16


def bf(x):
    return np.asarray(x, np.float32).astype(BF16)


def f64(x):
    return np.asarray(x).astype(np.float64)


L, D, HQ, HKV, HD, WIN, ROPE_BASE = 512, 2048, 16, 4, 128, 256, 1024
HALF = HD // 2
QUART = HALF // 2
NQ = HQ * HD
NKV = HKV * HD


def rope_tables():
    freqs = (1.0 / ROPE_BASE) ** np.linspace(0.0, 1.0, num=QUART)
    freqs = np.concatenate([freqs, np.zeros(QUART)])
    theta = np.arange(L, dtype=np.float64)[:, None] * freqs[None, :]
    return np.cos(theta)[:, None, :], np.sin(theta)[:, None, :]


def rotate(u, cos, sin):
    u1, u2 = u[..., :HALF], u[..., HALF:]
    return np.concatenate([u1 * cos + u2 * sin, -u1 * sin + u2 * cos], axis=-1)


def setup_inputs():
    s = mx_kscale(D)
    return {"x": bf(np.random.standard_normal((L, D)) * s),
            "Wqkv": bf(np.random.standard_normal((D, NQ + NKV + NKV)) * 1.25 / np.sqrt(D) / s[:, None])}


def reference(x, Wqkv):
    proj = mxq(f64(x), 1, "e5m2") @ mxq(f64(Wqkv), 0, "e5m2")
    q = proj[:, :NQ].reshape(L, HQ, HD)
    k = proj[:, NQ:NQ + NKV].reshape(L, HKV, HD)
    v = proj[:, NQ + NKV:].reshape(L, HKV, HD)
    cos, sin = rope_tables()
    return rotate(q, cos, sin), rotate(k, cos, sin), v

@@ -1,0 +1,232 @@
+from contextlib import ExitStack
+import math
+
+import concourse.mybir as mybir
+from concourse.masks import make_identity
+
+L, D, NOUT = 512, 2048, 3072
+FLOPS = 2 * L * D * NOUT
+
+F32 = mybir.dt.float32
+BF16 = mybir.dt.bfloat16
+U32 = mybir.dt.uint32
+U8 = mybir.dt.uint8
+I32 = mybir.dt.int32
+FP8X4 = mybir.dt.float8_e5m2_x4
+ALU = mybir.AluOpType
+ACT = mybir.ActivationFunctionType
+
+P = 128
+PACK = 4
+K_PASS = P * PACK
+PASSES = D // K_PASS
+MT = L // P
+BANK = 512
+CG_COLS = 1024
+NCG = NOUT // CG_COLS
+NF = 32
+UNIT = 32
+UNITS = CG_COLS // UNIT
+
+S_UNITS = [[16, 16, 16, 16], [20, 20, 20, 20], [20, 20, 22, 22]]
+NEG_STEP = True
+
+
+def tile_groupedqueryattention_pa_kernel(tc, x, Wqkv, out_0, out_1, out_2):
+    nc = tc.nc
+    with ExitStack() as ctx:
+        const = ctx.enter_context(tc.tile_pool(name="const", bufs=1))
+        xin = ctx.enter_context(tc.tile_pool(name="xin", bufs=MT))
+        xstage = ctx.enter_context(tc.tile_pool(name="xstage", bufs=2))
+        win = ctx.enter_context(tc.tile_pool(name="win", bufs=10))
+        wstage = ctx.enter_context(tc.tile_pool(name="wstage", bufs=3))
+        wcodes = ctx.enter_context(tc.tile_pool(name="wcodes", bufs=8))
+        outp = ctx.enter_context(tc.tile_pool(name="outp", bufs=4))
+        tmp = ctx.enter_context(tc.tile_pool(name="tmp", bufs=2))
+        psum = ctx.enter_context(tc.psum_pool(name="psum", bufs=8))
+
+        x_raw = []
+        w_raw = {}
+
+        def load_x(m):
+            xr = xin.tile([P, D], BF16, name="xr")
+            nc.sync.dma_start(out=xr[:], in_=x[m * P:(m + 1) * P, :])
+            x_raw.append(xr)
+
+        def load_w(cg, g):
+            wr = win.tile([P, PACK, CG_COLS], BF16, name="wr")
+            nc.sync.dma_start(
+                out=wr[:],
+                in_=Wqkv[g * K_PASS:(g + 1) * K_PASS, cg * CG_COLS:(cg + 1) * CG_COLS].rearrange(
+                    "(p j) w -> p j w", j=PACK),
+            )
+            w_raw[(cg, g)] = wr
+
+        load_x(0)
+        load_w(0, 0)
+        load_x(1)
+        load_x(2)
+        load_x(3)
+        for g in range(1, PASSES):
+            load_w(0, g)
+        for cg in range(1, NCG):
+            for g in range(PASSES):
+                load_w(cg, g)
+
+        ident = const.tile([P, P], F32, name="ident")
+        make_identity(nc, ident[:])
+
+        ones = const.tile([P, 1], F32, name="ones")
+        nc.vector.memset(ones[:], 1.0)
+        pos = const.tile([P, MT], F32, name="pos")
+        nc.gpsimd.iota(pos[:], pattern=[[P, MT]], base=0, channel_multiplier=1,
+                       allow_small_or_imprecise_dtypes=True)
+        turns = const.tile([P, NF], F32, name="turns")
+        nc.vector.tensor_scalar(out=turns[:, 0:1], in0=ones[:], scalar1=1.0 / (2.0 * math.pi),
+                                scalar2=None, op0=ALU.mult)
+        ratio = (1.0 / 1024.0) ** (1.0 / 31.0)
+        for b in range(5):
+            n = 2 ** b
+            nc.vector.tensor_scalar(out=turns[:, n:2 * n], in0=turns[:, 0:n], scalar1=ratio ** n,
+                                    scalar2=None, op0=ALU.mult)
+        TW = MT * NF
+        y = const.tile([P, MT, NF], F32, name="y")
+        nc.vector.tensor_tensor(out=y[:], in0=pos[:].unsqueeze(2).to_broadcast([P, MT, NF]),
+                                in1=turns[:].unsqueeze(1).to_broadcast([P, MT, NF]), op=ALU.mult)
+        ki = const.tile([P, TW], I32, name="ki")
+        yf = y[:].rearrange("p m f -> p (m f)")
+        nc.vector.tensor_copy(out=ki[:], in_=yf)
+        kf = const.tile([P, TW], F32, name="kf")
+        nc.vector.tensor_copy(out=kf[:], in_=ki[:])
+        fr = const.tile([P, TW], F32, name="fr")
+        nc.vector.tensor_tensor(out=fr[:], in0=yf, in1=kf[:], op=ALU.subtract)
+        wneg = const.tile([P, MT, NF], F32, name="wneg")
+        wnf = wneg[:].rearrange("p m f -> p (m f)")
+        nc.vector.scalar_tensor_tensor(out=wnf, in0=fr[:], scalar=0.5, in1=fr[:],
+                                       op0=ALU.is_gt, op1=ALU.subtract)
+        wabs = const.tile([P, MT, NF], F32, name="wabs")
+        nc.vector.scalar_tensor_tensor(out=wabs[:].rearrange("p m f -> p (m f)"), in0=wnf, scalar=-1.0,
+                                       in1=wnf, op0=ALU.mult, op1=ALU.max)
+        sin_t = const.tile([P, MT, 2, NF], F32, name="sin_t")
+        cos_t = const.tile([P, MT, NF], F32, name="cos_t")
+        nc.scalar.activation(out=sin_t[:, :, 0, :], in_=wneg[:], func=ACT.Sin, scale=2.0 * math.pi)
+        nc.scalar.activation(out=sin_t[:, :, 1, :], in_=wneg[:], func=ACT.Sin, scale=-2.0 * math.pi)
+        nc.scalar.activation(out=cos_t[:], in_=wabs[:], func=ACT.Sin, scale=-2.0 * math.pi,
+                             bias=math.pi / 2.0)
+
+        xq = const.tile([P, MT * PASSES * P], U32, name="xq", align_bytes=64)
+        xs = const.tile([P, MT * PASSES * P], U8, name="xs", align_bytes=64)
+        for m in range(MT):
+            words = x_raw[m][:].bitcast(F32)
+            xg = xstage.tile([P, PASSES * P * PACK], BF16, name="xg", align_bytes=64)
+            xgw = xg[:].bitcast(F32)
+            for b in range(2):
+                xt = psum.tile([P, BANK], F32, name="bank")
+                for gg in range(2):
+                    g = 2 * b + gg
+                    for u in range(2):
+                        s = 2 * gg + u
+                        nc.tensor.transpose(xt[:, s * P:(s + 1) * P],
+                                            words[:, 256 * g + u:256 * (g + 1):2], ident[:])
+                dst = xgw[:, BANK * b:BANK * (b + 1)].rearrange("p (g r u) -> p g r u", g=2, u=2)
+                src = xt[:].rearrange("p (g u r) -> p g r u", g=2, u=2)
+                if b == 0:
+                    nc.scalar.copy(out=dst, in_=src)
+                else:
+                    nc.vector.tensor_copy(out=dst, in_=src)
+            w0 = m * PASSES * P
+            nc.vector.quantize_mx(out=xq[:, w0:w0 + PASSES * P].bitcast(FP8X4),
+                                  scales=xs[:, w0:w0 + PASSES * P], in_=xg[:])
+
+        def segments(cg, wr, wg):
+            if cg < 2:
+                src = wr[:].rearrange("p j (a y c) -> p y a c j", y=2, c=UNIT)
+                dst = wg[:].rearrange("p (y a c j) -> p y a c j", y=2, c=UNIT, j=PACK)
+                return [(0, 16, dst[:, 0], src[:, 0]), (16, 16, dst[:, 1], src[:, 1])]
+            srck = wr[:, :, 0:BANK].rearrange("p j (a y c) -> p y a c j", y=2, c=UNIT)
+            dstk = wg[:, 0:BANK * PACK].rearrange("p (y a c j) -> p y a c j", y=2, c=UNIT, j=PACK)
+            srcv = wr[:, :, BANK:2 * BANK].rearrange("p j (a c) -> p a c j", c=UNIT)
+            dstv = wg[:, BANK * PACK:2 * BANK * PACK].rearrange("p (a c j) -> p a c j", c=UNIT, j=PACK)
+            return [(0, 8, dstk[:, 0], srck[:, 0]), (8, 8, dstk[:, 1], srck[:, 1]), (16, 16, dstv, srcv)]
+
+        def prep_w(cg, g):
+            wr = w_raw[(cg, g)]
+            wg = wstage.tile([P, CG_COLS * PACK], BF16, name="wg", align_bytes=64)
+            n_s = S_UNITS[cg][g]
+            for (u0, nu, dst, src) in segments(cg, wr, wg):
+                cut = min(max(n_s - u0, 0), nu)
+                if cut > 0:
+                    nc.scalar.copy(out=dst[:, 0:cut], in_=src[:, 0:cut])
+                if cut < nu:
+                    nc.vector.tensor_copy(out=dst[:, cut:nu], in_=src[:, cut:nu])
+            wq = wcodes.tile([P, CG_COLS], U32, name="wq", align_bytes=64)
+            ws = wcodes.tile([P, CG_COLS], U8, name="ws", align_bytes=64)
+            nc.vector.quantize_mx(out=wq[:].bitcast(FP8X4), scales=ws[:], in_=wg[:])
+            return wq, ws
+
+        out0v = out_0.rearrange("l h d -> l (h d)")
+        out1v = out_1.rearrange("l h d -> l (h d)")
+        out2v = out_2.rearrange("l h d -> l (h d)")
+
+        def rope(acc_rot, width, m, o_rot):
+            nh = width // (2 * NF)
+            t1 = tmp.tile([P, BANK], F32, name="t1")
+            t2 = tmp.tile([P, BANK], F32, name="t2")
+            nc.vector.tensor_tensor(
+                out=t1[:, 0:width].rearrange("p (a c) -> p a c", c=NF),
+                in0=acc_rot.rearrange("p (a c) -> p a c", c=NF),
+                in1=cos_t[:, m, :].unsqueeze(1).to_broadcast([P, 2 * nh, NF]), op=ALU.mult)
+            nc.vector.tensor_tensor(
+                out=t2[:, 0:width].rearrange("p (h c) -> p h c", c=2 * NF),
+                in0=acc_rot.rearrange("p (h c) -> p h c", c=2 * NF),
+                in1=sin_t[:, m].rearrange("p s c -> p (s c)").unsqueeze(1).to_broadcast([P, nh, 2 * NF]),
+                op=ALU.mult)
+            t1v = t1[:, 0:width].rearrange("p (h s c) -> p h s c", s=2, c=NF)
+            t2v = t2[:, 0:width].rearrange("p (h s c) -> p h s c", s=2, c=NF)
+            if NEG_STEP:
+                nc.vector.tensor_tensor(out=o_rot, in0=t1v, in1=t2v[:, :, ::-1, :], op=ALU.add)
+            else:
+                for s in range(2):
+                    nc.vector.tensor_tensor(out=o_rot[:, :, s, :], in0=t1v[:, :, s, :],
+                                            in1=t2v[:, :, 1 - s, :], op=ALU.add)
+
+        def epilogue(cg, m, acc0, acc1):
+            o = outp.tile([P, CG_COLS], F32, name="o")
+            rows = slice(m * P, (m + 1) * P)
+            if cg < 2:
+                ov = o[:].rearrange("p (h s y c) -> p y h s c", s=2, y=2, c=NF)
+                nc.scalar.copy(out=o[:].rearrange("p (a y c) -> p y a c", y=2, c=NF)[:, 1],
+                               in_=acc1[:].rearrange("p (a c) -> p a c", c=NF))
+                rope(acc0[:], BANK, m, ov[:, 0])
+                nc.sync.dma_start(out=out0v[rows, cg * CG_COLS:(cg + 1) * CG_COLS], in_=o[:])
+            else:
+                half = BANK // 2
+                ov = o[:, 0:BANK].rearrange("p (h s y c) -> p y h s c", s=2, y=2, c=NF)
+                nc.scalar.copy(out=o[:, BANK:2 * BANK], in_=acc1[:])
+                nc.sync.dma_start(out=out2v[rows, :], in_=o[:, BANK:2 * BANK])
+                rope(acc0[:, 0:half], half, m, ov[:, 0])
+                nc.scalar.copy(out=o[:, 0:BANK].rearrange("p (a y c) -> p y a c", y=2, c=NF)[:, 1],
+                               in_=acc0[:, half:BANK].rearrange("p (a c) -> p a c", c=NF))
+                nc.sync.dma_start(out=out1v[rows, :], in_=o[:, 0:BANK])
+
+        for cg in range(NCG):
+            acc = {}
+            for g in range(PASSES):
+                wq, ws = prep_w(cg, g)
+                for m in range(MT):
+                    w0 = (m * PASSES + g) * P
+                    for yb in range(2):
+                        if g == 0:
+                            bank = psum.tile([P, BANK], F32, name="bank")
+                            acc[(m, yb)] = bank
+                        nc.tensor.matmul_mx(
+                            out=acc[(m, yb)][:],
+                            lhsT=xq[:, w0:w0 + P].bitcast(FP8X4),
+                            lhsT_scale=xs[:, w0:w0 + P],
+                            rhs=wq[:, yb * BANK:(yb + 1) * BANK].bitcast(FP8X4),
+                            rhs_scale=ws[:, yb * BANK:(yb + 1) * BANK],
+                            start=(g == 0),
+                            stop=(g == PASSES - 1),
+                        )
+            for m in range(MT):
+                epilogue(cg, m, acc[(m, 0)], acc[(m, 1)])

@@ -28,8 +28,8 @@ NF = 32
 UNIT = 32
 UNITS = CG_COLS // UNIT
 
-S_UNITS = [[16, 16, 16, 16], [20, 20, 20, 20], [20, 20, 22, 22]]
-NEG_STEP = True
+S_UNITS = [[8, 6], [12, 12], [10, 12]]
+G_ADD = False
 
 
 def tile_groupedqueryattention_pa_kernel(tc, x, Wqkv, out_0, out_1, out_2):
@@ -38,12 +38,13 @@ def tile_groupedqueryattention_pa_kernel(tc, x, Wqkv, out_0, out_1, out_2):
         const = ctx.enter_context(tc.tile_pool(name="const", bufs=1))
         xin = ctx.enter_context(tc.tile_pool(name="xin", bufs=MT))
         xstage = ctx.enter_context(tc.tile_pool(name="xstage", bufs=2))
-        win = ctx.enter_context(tc.tile_pool(name="win", bufs=10))
-        wstage = ctx.enter_context(tc.tile_pool(name="wstage", bufs=3))
-        wcodes = ctx.enter_context(tc.tile_pool(name="wcodes", bufs=8))
-        outp = ctx.enter_context(tc.tile_pool(name="outp", bufs=4))
-        tmp = ctx.enter_context(tc.tile_pool(name="tmp", bufs=2))
+        win = ctx.enter_context(tc.tile_pool(name="win", bufs=8))
+        wstage = ctx.enter_context(tc.tile_pool(name="wstage", bufs=8))
+        wcodes = ctx.enter_context(tc.tile_pool(name="wcodes", bufs=16))
+        outp = ctx.enter_context(tc.tile_pool(name="outp", bufs=8))
+        tmp = ctx.enter_context(tc.tile_pool(name="tmp", bufs=3))
         psum = ctx.enter_context(tc.psum_pool(name="psum", bufs=8))
+        ctx.enter_context(tc.manual_schedule())
 
         x_raw = []
         w_raw = {}
@@ -62,16 +63,14 @@ def tile_groupedqueryattention_pa_kernel(tc, x, Wqkv, out_0, out_1, out_2):
             )
             w_raw[(cg, g)] = wr
 
-        load_x(0)
         load_w(0, 0)
+        load_x(0)
         load_x(1)
+        load_w(0, 1)
         load_x(2)
         load_x(3)
-        for g in range(1, PASSES):
-            load_w(0, g)
-        for cg in range(1, NCG):
-            for g in range(PASSES):
-                load_w(cg, g)
+        for i in range(2, NCG * PASSES):
+            load_w(i // PASSES, i % PASSES)
 
         ident = const.tile([P, P], F32, name="ident")
         make_identity(nc, ident[:])
@@ -116,9 +115,12 @@ def tile_groupedqueryattention_pa_kernel(tc, x, Wqkv, out_0, out_1, out_2):
 
         xq = const.tile([P, MT * PASSES * P], U32, name="xq", align_bytes=64)
         xs = const.tile([P, MT * PASSES * P], U8, name="xs", align_bytes=64)
-        for m in range(MT):
+        x_grouped = {}
+
+        def x_turn(m):
             words = x_raw[m][:].bitcast(F32)
             xg = xstage.tile([P, PASSES * P * PACK], BF16, name="xg", align_bytes=64)
+            x_grouped[m] = xg
             xgw = xg[:].bitcast(F32)
             for b in range(2):
                 xt = psum.tile([P, BANK], F32, name="bank")
@@ -128,48 +130,107 @@ def tile_groupedqueryattention_pa_kernel(tc, x, Wqkv, out_0, out_1, out_2):
                         s = 2 * gg + u
                         nc.tensor.transpose(xt[:, s * P:(s + 1) * P],
                                             words[:, 256 * g + u:256 * (g + 1):2], ident[:])
-                dst = xgw[:, BANK * b:BANK * (b + 1)].rearrange("p (g r u) -> p g r u", g=2, u=2)
-                src = xt[:].rearrange("p (g u r) -> p g r u", g=2, u=2)
-                if b == 0:
-                    nc.scalar.copy(out=dst, in_=src)
-                else:
-                    nc.vector.tensor_copy(out=dst, in_=src)
+                nc.scalar.copy(out=xgw[:, BANK * b:BANK * (b + 1)].rearrange("p (g r u) -> p g r u", g=2, u=2),
+                               in_=xt[:].rearrange("p (g u r) -> p g r u", g=2, u=2))
+
+        def x_quant(m):
             w0 = m * PASSES * P
             nc.vector.quantize_mx(out=xq[:, w0:w0 + PASSES * P].bitcast(FP8X4),
-                                  scales=xs[:, w0:w0 + PASSES * P], in_=xg[:])
+                                  scales=xs[:, w0:w0 + PASSES * P], in_=x_grouped[m][:])
 
-        def segments(cg, wr, wg):
+        SRC_RU = "p j (a y b i) -> p y a b j i"
+        SRC_V = "p j (a b i) -> p a b j i"
+        DST = "p (a b i j) -> p a b j i"
+        NB = UNIT // 4
+
+        def segments(cg, h, wr, wg):
             if cg < 2:
-                src = wr[:].rearrange("p j (a y c) -> p y a c j", y=2, c=UNIT)
-                dst = wg[:].rearrange("p (y a c j) -> p y a c j", y=2, c=UNIT, j=PACK)
-                return [(0, 16, dst[:, 0], src[:, 0]), (16, 16, dst[:, 1], src[:, 1])]
-            srck = wr[:, :, 0:BANK].rearrange("p j (a y c) -> p y a c j", y=2, c=UNIT)
-            dstk = wg[:, 0:BANK * PACK].rearrange("p (y a c j) -> p y a c j", y=2, c=UNIT, j=PACK)
-            srcv = wr[:, :, BANK:2 * BANK].rearrange("p j (a c) -> p a c j", c=UNIT)
-            dstv = wg[:, BANK * PACK:2 * BANK * PACK].rearrange("p (a c j) -> p a c j", c=UNIT, j=PACK)
-            return [(0, 8, dstk[:, 0], srck[:, 0]), (8, 8, dstk[:, 1], srck[:, 1]), (16, 16, dstv, srcv)]
+                return [(0, 16, wg[:].rearrange(DST, b=NB, i=4, j=PACK),
+                         wr[:].rearrange(SRC_RU, y=2, b=NB, i=4)[:, h])]
+            if h == 0:
+                srck = wr[:, :, 0:BANK].rearrange(SRC_RU, y=2, b=NB, i=4)
+                half = BANK * PACK // 2
+                return [(0, 8, wg[:, 0:half].rearrange(DST, b=NB, i=4, j=PACK), srck[:, 0]),
+                        (8, 8, wg[:, half:2 * half].rearrange(DST, b=NB, i=4, j=PACK), srck[:, 1])]
+            return [(0, 16, wg[:].rearrange(DST, b=NB, i=4, j=PACK),
+                     wr[:, :, BANK:2 * BANK].rearrange(SRC_V, b=NB, i=4))]
 
-        def prep_w(cg, g):
-            wr = w_raw[(cg, g)]
-            wg = wstage.tile([P, CG_COLS * PACK], BF16, name="wg", align_bytes=64)
-            n_s = S_UNITS[cg][g]
-            for (u0, nu, dst, src) in segments(cg, wr, wg):
+        w_grouped = {}
+        w_codes = {}
+
+        def w_copy(i, h):
+            cg, g = divmod(i, PASSES)
+            wg = wstage.tile([P, BANK * PACK], BF16, name="wg", align_bytes=64)
+            w_grouped[(i, h)] = wg
+            n_s = S_UNITS[cg][h]
+            segs = segments(cg, h, w_raw[(cg, g)], wg)
+            for (u0, nu, dst, src) in segs:
                 cut = min(max(n_s - u0, 0), nu)
                 if cut > 0:
                     nc.scalar.copy(out=dst[:, 0:cut], in_=src[:, 0:cut])
+            for (u0, nu, dst, src) in segs:
+                cut = min(max(n_s - u0, 0), nu)
                 if cut < nu:
                     nc.vector.tensor_copy(out=dst[:, cut:nu], in_=src[:, cut:nu])
-            wq = wcodes.tile([P, CG_COLS], U32, name="wq", align_bytes=64)
-            ws = wcodes.tile([P, CG_COLS], U8, name="ws", align_bytes=64)
-            nc.vector.quantize_mx(out=wq[:].bitcast(FP8X4), scales=ws[:], in_=wg[:])
-            return wq, ws
+
+        def w_quant(i, h):
+            wq = wcodes.tile([P, BANK], U32, name="wq", align_bytes=64)
+            ws = wcodes.tile([P, BANK], U8, name="ws", align_bytes=64)
+            nc.vector.quantize_mx(out=wq[:].bitcast(FP8X4), scales=ws[:], in_=w_grouped[(i, h)][:])
+            w_codes[(i, h)] = (wq, ws)
+
+        acc = {}
+
+        def passes(i, h):
+            cg, g = divmod(i, PASSES)
+            wq, ws = w_codes[(i, h)]
+            for m in range(MT):
+                w0 = (m * PASSES + g) * P
+                if g == 0:
+                    bank = psum.tile([P, BANK], F32, name="bank")
+                    acc[(cg, h, m)] = bank
+                nc.tensor.matmul_mx(
+                    out=acc[(cg, h, m)][:],
+                    lhsT=xq[:, w0:w0 + P].bitcast(FP8X4), lhsT_scale=xs[:, w0:w0 + P],
+                    rhs=wq[:].bitcast(FP8X4), rhs_scale=ws[:],
+                    start=(g == 0), stop=(g == PASSES - 1))
 
         out0v = out_0.rearrange("l h d -> l (h d)")
         out1v = out_1.rearrange("l h d -> l (h d)")
         out2v = out_2.rearrange("l h d -> l (h d)")
+        prods = {}
+        o_tiles = {}
 
-        def rope(acc_rot, width, m, o_rot):
+        def o_tile(cg, m):
+            if (cg, m) not in o_tiles:
+                o = outp.tile([P, CG_COLS], F32, name="o")
+                o_tiles[(cg, m)] = o
+            return o_tiles[(cg, m)]
+
+        def plain_copy(cg, m, eng_is_vector=False):
+            o = o_tile(cg, m)
+            if cg < 2:
+                dst = o[:].rearrange("p (a y c) -> p y a c", y=2, c=NF)[:, 1]
+                src = acc[(cg, 1, m)][:].rearrange("p (a c) -> p a c", c=NF)
+            else:
+                dst = o[:, BANK:2 * BANK]
+                src = acc[(cg, 1, m)][:]
+            if eng_is_vector:
+                nc.vector.tensor_copy(out=dst, in_=src)
+            else:
+                nc.scalar.copy(out=dst, in_=src)
+            if cg == 2:
+                nc.sync.dma_start(out=out2v[m * P:(m + 1) * P, :], in_=o[:, BANK:2 * BANK])
+
+        def k_plain_copy(m):
+            o = o_tile(2, m)
+            nc.scalar.copy(out=o[:, 0:BANK].rearrange("p (a y c) -> p y a c", y=2, c=NF)[:, 1],
+                           in_=acc[(2, 0, m)][:, BANK // 2:BANK].rearrange("p (a c) -> p a c", c=NF))
+
+        def rope_mults(cg, m):
+            width = BANK if cg < 2 else BANK // 2
             nh = width // (2 * NF)
+            acc_rot = acc[(cg, 0, m)][:, 0:width]
             t1 = tmp.tile([P, BANK], F32, name="t1")
             t2 = tmp.tile([P, BANK], F32, name="t2")
             nc.vector.tensor_tensor(
@@ -181,52 +242,101 @@ def tile_groupedqueryattention_pa_kernel(tc, x, Wqkv, out_0, out_1, out_2):
                 in0=acc_rot.rearrange("p (h c) -> p h c", c=2 * NF),
                 in1=sin_t[:, m].rearrange("p s c -> p (s c)").unsqueeze(1).to_broadcast([P, nh, 2 * NF]),
                 op=ALU.mult)
-            t1v = t1[:, 0:width].rearrange("p (h s c) -> p h s c", s=2, c=NF)
-            t2v = t2[:, 0:width].rearrange("p (h s c) -> p h s c", s=2, c=NF)
-            if NEG_STEP:
-                nc.vector.tensor_tensor(out=o_rot, in0=t1v, in1=t2v[:, :, ::-1, :], op=ALU.add)
-            else:
-                for s in range(2):
-                    nc.vector.tensor_tensor(out=o_rot[:, :, s, :], in0=t1v[:, :, s, :],
-                                            in1=t2v[:, :, 1 - s, :], op=ALU.add)
+            prods[(cg, m)] = (t1[:, 0:width].rearrange("p (h s c) -> p h s c", s=2, c=NF),
+                              t2[:, 0:width].rearrange("p (h s c) -> p h s c", s=2, c=NF))
 
-        def epilogue(cg, m, acc0, acc1):
-            o = outp.tile([P, CG_COLS], F32, name="o")
+        def rope_add_store(cg, m):
+            t1v, t2v = prods[(cg, m)]
+            o = o_tile(cg, m)
             rows = slice(m * P, (m + 1) * P)
+            width = CG_COLS if cg < 2 else BANK
+            o_rot = o[:, 0:width].rearrange("p (h s y c) -> p y h s c", s=2, y=2, c=NF)[:, 0]
+            eng = nc.gpsimd if G_ADD else nc.vector
+            eng.tensor_tensor(out=o_rot, in0=t1v, in1=t2v[:, :, ::-1, :], op=ALU.add)
             if cg < 2:
-                ov = o[:].rearrange("p (h s y c) -> p y h s c", s=2, y=2, c=NF)
-                nc.scalar.copy(out=o[:].rearrange("p (a y c) -> p y a c", y=2, c=NF)[:, 1],
-                               in_=acc1[:].rearrange("p (a c) -> p a c", c=NF))
-                rope(acc0[:], BANK, m, ov[:, 0])
                 nc.sync.dma_start(out=out0v[rows, cg * CG_COLS:(cg + 1) * CG_COLS], in_=o[:])
             else:
-                half = BANK // 2
-                ov = o[:, 0:BANK].rearrange("p (h s y c) -> p y h s c", s=2, y=2, c=NF)
-                nc.scalar.copy(out=o[:, BANK:2 * BANK], in_=acc1[:])
-                nc.sync.dma_start(out=out2v[rows, :], in_=o[:, BANK:2 * BANK])
-                rope(acc0[:, 0:half], half, m, ov[:, 0])
-                nc.scalar.copy(out=o[:, 0:BANK].rearrange("p (a y c) -> p y a c", y=2, c=NF)[:, 1],
-                               in_=acc0[:, half:BANK].rearrange("p (a c) -> p a c", c=NF))
                 nc.sync.dma_start(out=out1v[rows, :], in_=o[:, 0:BANK])
 
-        for cg in range(NCG):
-            acc = {}
-            for g in range(PASSES):
-                wq, ws = prep_w(cg, g)
-                for m in range(MT):
-                    w0 = (m * PASSES + g) * P
-                    for yb in range(2):
-                        if g == 0:
-                            bank = psum.tile([P, BANK], F32, name="bank")
-                            acc[(m, yb)] = bank
-                        nc.tensor.matmul_mx(
-                            out=acc[(m, yb)][:],
-                            lhsT=xq[:, w0:w0 + P].bitcast(FP8X4),
-                            lhsT_scale=xs[:, w0:w0 + P],
-                            rhs=wq[:, yb * BANK:(yb + 1) * BANK].bitcast(FP8X4),
-                            rhs_scale=ws[:, yb * BANK:(yb + 1) * BANK],
-                            start=(g == 0),
-                            stop=(g == PASSES - 1),
-                        )
+        def copy2(i):
+            w_copy(i, 0)
+            w_copy(i, 1)
+
+        def quant_mm(i, h):
+            w_quant(i, h)
+            passes(i, h)
+
+        def quant_mm2(i):
+            quant_mm(i, 0)
+            quant_mm(i, 1)
+
+        def q_epilogue(cg, fillers):
             for m in range(MT):
-                epilogue(cg, m, acc[(m, 0)], acc[(m, 1)])
+                plain_copy(cg, m)
+                rope_mults(cg, m)
+                if m >= 1:
+                    rope_add_store(cg, m - 1)
+            for (i, h) in fillers:
+                w_copy(i, h)
+            rope_add_store(cg, MT - 1)
+
+        copy2(0)
+        x_turn(0)
+        w_quant(0, 0)
+        w_quant(0, 1)
+        x_quant(0)
+        x_turn(1)
+        x_quant(1)
+        copy2(1)
+        x_turn(2)
+        w_quant(1, 0)
+        w_quant(1, 1)
+        x_quant(2)
+        x_turn(3)
+        x_quant(3)
+        for i in range(2):
+            passes(i, 0)
+            passes(i, 1)
+        for i in range(2, 4):
+            copy2(i)
+            quant_mm2(i)
+        copy2(4)
+        q_epilogue(0, [(5, 0), (5, 1)])
+        quant_mm2(4)
+        copy2(6)
+        quant_mm2(5)
+        copy2(7)
+        quant_mm2(6)
+        w_copy(8, 0)
+        quant_mm2(7)
+        w_copy(9, 0)
+        q_epilogue(1, [(10, 0)])
+        quant_mm(8, 0)
+        w_copy(11, 0)
+        quant_mm(9, 0)
+        w_copy(8, 1)
+        quant_mm(10, 0)
+        w_copy(9, 1)
+        quant_mm(11, 0)
+        w_copy(10, 1)
+        quant_mm(8, 1)
+        rope_mults(2, 0)
+        k_plain_copy(0)
+        w_copy(11, 1)
+        quant_mm(9, 1)
+        rope_mults(2, 1)
+        k_plain_copy(1)
+        rope_add_store(2, 0)
+        quant_mm(10, 1)
+        rope_mults(2, 2)
+        k_plain_copy(2)
+        rope_add_store(2, 1)
+        quant_mm(11, 1)
+        rope_mults(2, 3)
+        k_plain_copy(3)
+        rope_add_store(2, 2)
+        plain_copy(2, 0)
+        plain_copy(2, 2, True)
+        rope_add_store(2, 3)
+        plain_copy(2, 1)
+        plain_copy(2, 3, True)

@@ -28,8 +28,9 @@ NF = 32
 UNIT = 32
 UNITS = CG_COLS // UNIT
 
-S_UNITS = [[8, 6], [12, 12], [10, 12]]
-G_ADD = False
+S_UNITS = [[8, 6], [10, 14], [8, 16]]
+G_ADD = True
+V_PLAIN = 2
 
 
 def tile_groupedqueryattention_pa_kernel(tc, x, Wqkv, out_0, out_1, out_2):
@@ -42,7 +43,7 @@ def tile_groupedqueryattention_pa_kernel(tc, x, Wqkv, out_0, out_1, out_2):
         wstage = ctx.enter_context(tc.tile_pool(name="wstage", bufs=8))
         wcodes = ctx.enter_context(tc.tile_pool(name="wcodes", bufs=16))
         outp = ctx.enter_context(tc.tile_pool(name="outp", bufs=8))
-        tmp = ctx.enter_context(tc.tile_pool(name="tmp", bufs=3))
+        tmp = ctx.enter_context(tc.tile_pool(name="tmp", bufs=4))
         psum = ctx.enter_context(tc.psum_pool(name="psum", bufs=8))
         ctx.enter_context(tc.manual_schedule())
 
@@ -245,14 +246,17 @@ def tile_groupedqueryattention_pa_kernel(tc, x, Wqkv, out_0, out_1, out_2):
             prods[(cg, m)] = (t1[:, 0:width].rearrange("p (h s c) -> p h s c", s=2, c=NF),
                               t2[:, 0:width].rearrange("p (h s c) -> p h s c", s=2, c=NF))
 
-        def rope_add_store(cg, m):
+        def rope_add(cg, m):
             t1v, t2v = prods[(cg, m)]
             o = o_tile(cg, m)
-            rows = slice(m * P, (m + 1) * P)
             width = CG_COLS if cg < 2 else BANK
             o_rot = o[:, 0:width].rearrange("p (h s y c) -> p y h s c", s=2, y=2, c=NF)[:, 0]
-            eng = nc.gpsimd if G_ADD else nc.vector
+            eng = nc.gpsimd if (G_ADD and cg < 2) else nc.vector
             eng.tensor_tensor(out=o_rot, in0=t1v, in1=t2v[:, :, ::-1, :], op=ALU.add)
+
+        def store(cg, m):
+            o = o_tile(cg, m)
+            rows = slice(m * P, (m + 1) * P)
             if cg < 2:
                 nc.sync.dma_start(out=out0v[rows, cg * CG_COLS:(cg + 1) * CG_COLS], in_=o[:])
             else:
@@ -271,14 +275,18 @@ def tile_groupedqueryattention_pa_kernel(tc, x, Wqkv, out_0, out_1, out_2):
             quant_mm(i, 1)
 
         def q_epilogue(cg, fillers):
-            for m in range(MT):
+            for m in range(MT - V_PLAIN):
                 plain_copy(cg, m)
+            for m in range(MT):
                 rope_mults(cg, m)
-                if m >= 1:
-                    rope_add_store(cg, m - 1)
+                rope_add(cg, m)
+                if m < MT - V_PLAIN:
+                    store(cg, m)
+            for m in range(MT - V_PLAIN, MT):
+                plain_copy(cg, m, True)
+                store(cg, m)
             for (i, h) in fillers:
                 w_copy(i, h)
-            rope_add_store(cg, MT - 1)
 
         copy2(0)
         x_turn(0)
@@ -307,36 +315,32 @@ def tile_groupedqueryattention_pa_kernel(tc, x, Wqkv, out_0, out_1, out_2):
         quant_mm2(5)
         copy2(7)
         quant_mm2(6)
-        w_copy(8, 0)
-        quant_mm2(7)
-        w_copy(9, 0)
-        q_epilogue(1, [(10, 0)])
-        quant_mm(8, 0)
-        w_copy(11, 0)
-        quant_mm(9, 0)
         w_copy(8, 1)
-        quant_mm(10, 0)
+        quant_mm2(7)
         w_copy(9, 1)
-        quant_mm(11, 0)
-        w_copy(10, 1)
+        q_epilogue(1, [(10, 1)])
         quant_mm(8, 1)
-        rope_mults(2, 0)
-        k_plain_copy(0)
         w_copy(11, 1)
         quant_mm(9, 1)
-        rope_mults(2, 1)
-        k_plain_copy(1)
-        rope_add_store(2, 0)
+        w_copy(8, 0)
         quant_mm(10, 1)
-        rope_mults(2, 2)
-        k_plain_copy(2)
-        rope_add_store(2, 1)
+        w_copy(9, 0)
         quant_mm(11, 1)
-        rope_mults(2, 3)
-        k_plain_copy(3)
-        rope_add_store(2, 2)
+        w_copy(10, 0)
+        quant_mm(8, 0)
         plain_copy(2, 0)
-        plain_copy(2, 2, True)
-        rope_add_store(2, 3)
+        w_copy(11, 0)
+        quant_mm(9, 0)
         plain_copy(2, 1)
-        plain_copy(2, 3, True)
+        quant_mm(10, 0)
+        plain_copy(2, 2)
+        quant_mm(11, 0)
+        plain_copy(2, 3)
+        for m in range(MT):
+            rope_mults(2, m)
+            k_plain_copy(m)
+            if m >= 1:
+                rope_add(2, m - 1)
+                store(2, m - 1)
+        rope_add(2, MT - 1)
+        store(2, MT - 1)

@@ -28,7 +28,7 @@ NF = 32
 UNIT = 32
 UNITS = CG_COLS // UNIT
 
-S_UNITS = [[8, 6], [10, 14], [8, 16]]
+S_UNITS = [[4, 8], [8, 10], [8, 12]]
 G_ADD = True
 V_PLAIN = 2
 

@@ -28,9 +28,8 @@ NF = 32
 UNIT = 32
 UNITS = CG_COLS // UNIT
 
-S_UNITS = [[4, 8], [8, 10], [8, 12]]
-G_ADD = True
-V_PLAIN = 2
+S_UNITS = [[8, 6], [12, 12], [10, 12]]
+G_ADD = False
 
 
 def tile_groupedqueryattention_pa_kernel(tc, x, Wqkv, out_0, out_1, out_2):
@@ -43,7 +42,7 @@ def tile_groupedqueryattention_pa_kernel(tc, x, Wqkv, out_0, out_1, out_2):
         wstage = ctx.enter_context(tc.tile_pool(name="wstage", bufs=8))
         wcodes = ctx.enter_context(tc.tile_pool(name="wcodes", bufs=16))
         outp = ctx.enter_context(tc.tile_pool(name="outp", bufs=8))
-        tmp = ctx.enter_context(tc.tile_pool(name="tmp", bufs=4))
+        tmp = ctx.enter_context(tc.tile_pool(name="tmp", bufs=3))
         psum = ctx.enter_context(tc.psum_pool(name="psum", bufs=8))
         ctx.enter_context(tc.manual_schedule())
 
@@ -139,9 +138,9 @@ def tile_groupedqueryattention_pa_kernel(tc, x, Wqkv, out_0, out_1, out_2):
             nc.vector.quantize_mx(out=xq[:, w0:w0 + PASSES * P].bitcast(FP8X4),
                                   scales=xs[:, w0:w0 + PASSES * P], in_=x_grouped[m][:])
 
-        SRC_RU = "p j (a y b i) -> p y a b j i"
-        SRC_V = "p j (a b i) -> p a b j i"
-        DST = "p (a b i j) -> p a b j i"
+        SRC_RU = "p j (a y b i) -> p y a b i j"
+        SRC_V = "p j (a b i) -> p a b i j"
+        DST = "p (a b i j) -> p a b i j"
         NB = UNIT // 4
 
         def segments(cg, h, wr, wg):
@@ -246,17 +245,14 @@ def tile_groupedqueryattention_pa_kernel(tc, x, Wqkv, out_0, out_1, out_2):
             prods[(cg, m)] = (t1[:, 0:width].rearrange("p (h s c) -> p h s c", s=2, c=NF),
                               t2[:, 0:width].rearrange("p (h s c) -> p h s c", s=2, c=NF))
 
-        def rope_add(cg, m):
+        def rope_add_store(cg, m):
             t1v, t2v = prods[(cg, m)]
             o = o_tile(cg, m)
+            rows = slice(m * P, (m + 1) * P)
             width = CG_COLS if cg < 2 else BANK
             o_rot = o[:, 0:width].rearrange("p (h s y c) -> p y h s c", s=2, y=2, c=NF)[:, 0]
-            eng = nc.gpsimd if (G_ADD and cg < 2) else nc.vector
+            eng = nc.gpsimd if G_ADD else nc.vector
             eng.tensor_tensor(out=o_rot, in0=t1v, in1=t2v[:, :, ::-1, :], op=ALU.add)
-
-        def store(cg, m):
-            o = o_tile(cg, m)
-            rows = slice(m * P, (m + 1) * P)
             if cg < 2:
                 nc.sync.dma_start(out=out0v[rows, cg * CG_COLS:(cg + 1) * CG_COLS], in_=o[:])
             else:
@@ -275,18 +271,14 @@ def tile_groupedqueryattention_pa_kernel(tc, x, Wqkv, out_0, out_1, out_2):
             quant_mm(i, 1)
 
         def q_epilogue(cg, fillers):
-            for m in range(MT - V_PLAIN):
-                plain_copy(cg, m)
             for m in range(MT):
+                plain_copy(cg, m)
                 rope_mults(cg, m)
-                rope_add(cg, m)
-                if m < MT - V_PLAIN:
-                    store(cg, m)
-            for m in range(MT - V_PLAIN, MT):
-                plain_copy(cg, m, True)
-                store(cg, m)
+                if m >= 1:
+                    rope_add_store(cg, m - 1)
             for (i, h) in fillers:
                 w_copy(i, h)
+            rope_add_store(cg, MT - 1)
 
         copy2(0)
         x_turn(0)
@@ -315,32 +307,36 @@ def tile_groupedqueryattention_pa_kernel(tc, x, Wqkv, out_0, out_1, out_2):
         quant_mm2(5)
         copy2(7)
         quant_mm2(6)
-        w_copy(8, 1)
-        quant_mm2(7)
-        w_copy(9, 1)
-        q_epilogue(1, [(10, 1)])
-        quant_mm(8, 1)
-        w_copy(11, 1)
-        quant_mm(9, 1)
         w_copy(8, 0)
-        quant_mm(10, 1)
+        quant_mm2(7)
         w_copy(9, 0)
-        quant_mm(11, 1)
-        w_copy(10, 0)
+        q_epilogue(1, [(10, 0)])
         quant_mm(8, 0)
-        plain_copy(2, 0)
         w_copy(11, 0)
         quant_mm(9, 0)
-        plain_copy(2, 1)
+        w_copy(8, 1)
         quant_mm(10, 0)
-        plain_copy(2, 2)
+        w_copy(9, 1)
         quant_mm(11, 0)
-        plain_copy(2, 3)
-        for m in range(MT):
-            rope_mults(2, m)
-            k_plain_copy(m)
-            if m >= 1:
-                rope_add(2, m - 1)
-                store(2, m - 1)
-        rope_add(2, MT - 1)
-        store(2, MT - 1)
+        w_copy(10, 1)
+        quant_mm(8, 1)
+        rope_mults(2, 0)
+        k_plain_copy(0)
+        w_copy(11, 1)
+        quant_mm(9, 1)
+        rope_mults(2, 1)
+        k_plain_copy(1)
+        rope_add_store(2, 0)
+        quant_mm(10, 1)
+        rope_mults(2, 2)
+        k_plain_copy(2)
+        rope_add_store(2, 1)
+        quant_mm(11, 1)
+        rope_mults(2, 3)
+        k_plain_copy(3)
+        rope_add_store(2, 2)
+        plain_copy(2, 0)
+        plain_copy(2, 2, True)
+        rope_add_store(2, 3)
+        plain_copy(2, 1)
+        plain_copy(2, 3, True)

@@ -28,8 +28,8 @@ NF = 32
 UNIT = 32
 UNITS = CG_COLS // UNIT
 
-S_UNITS = [[8, 6], [12, 12], [10, 12]]
-G_ADD = False
+S_UNITS = [[8, 6], [10, 10], [10, 12]]
+G_ADD = True
 
 
 def tile_groupedqueryattention_pa_kernel(tc, x, Wqkv, out_0, out_1, out_2):
@@ -251,7 +251,7 @@ def tile_groupedqueryattention_pa_kernel(tc, x, Wqkv, out_0, out_1, out_2):
             rows = slice(m * P, (m + 1) * P)
             width = CG_COLS if cg < 2 else BANK
             o_rot = o[:, 0:width].rearrange("p (h s y c) -> p y h s c", s=2, y=2, c=NF)[:, 0]
-            eng = nc.gpsimd if G_ADD else nc.vector
+            eng = nc.gpsimd if (G_ADD and cg < 2) else nc.vector
             eng.tensor_tensor(out=o_rot, in0=t1v, in1=t2v[:, :, ::-1, :], op=ALU.add)
             if cg < 2:
                 nc.sync.dma_start(out=out0v[rows, cg * CG_COLS:(cg + 1) * CG_COLS], in_=o[:])

@@ -29,7 +29,6 @@ UNIT = 32
 UNITS = CG_COLS // UNIT
 
 S_UNITS = [[8, 6], [10, 10], [10, 12]]
-G_ADD = True
 
 
 def tile_groupedqueryattention_pa_kernel(tc, x, Wqkv, out_0, out_1, out_2):
@@ -251,7 +250,7 @@ def tile_groupedqueryattention_pa_kernel(tc, x, Wqkv, out_0, out_1, out_2):
             rows = slice(m * P, (m + 1) * P)
             width = CG_COLS if cg < 2 else BANK
             o_rot = o[:, 0:width].rearrange("p (h s y c) -> p y h s c", s=2, y=2, c=NF)[:, 0]
-            eng = nc.gpsimd if (G_ADD and cg < 2) else nc.vector
+            eng = nc.gpsimd
             eng.tensor_tensor(out=o_rot, in0=t1v, in1=t2v[:, :, ::-1, :], op=ALU.add)
             if cg < 2:
                 nc.sync.dma_start(out=out0v[rows, cg * CG_COLS:(cg + 1) * CG_COLS], in_=o[:])

@@ -241,6 +241,9 @@ def tile_groupedqueryattention_pa_kernel(tc, x, Wqkv, out_0, out_1, out_2):
                 in0=acc_rot.rearrange("p (h c) -> p h c", c=2 * NF),
                 in1=sin_t[:, m].rearrange("p s c -> p (s c)").unsqueeze(1).to_broadcast([P, nh, 2 * NF]),
                 op=ALU.mult)
+            if cg < 2:
+                idle = psum.tile([P, BANK], F32, name="bank")
+                nc.tensor.matmul(out=idle[:], lhsT=ident[:], rhs=t1[:], start=True, stop=True)
             prods[(cg, m)] = (t1[:, 0:width].rearrange("p (h s c) -> p h s c", s=2, c=NF),
                               t2[:, 0:width].rearrange("p (h s c) -> p h s c", s=2, c=NF))
 

@@ -71,14 +71,15 @@ def tile_groupedqueryattention_pa_kernel(tc, x, Wqkv, out_0, out_1, out_2):
         for i in range(2, NCG * PASSES):
             load_w(i // PASSES, i % PASSES)
 
-        ident = const.tile([P, P], F32, name="ident")
-        make_identity(nc, ident[:])
-
         ones = const.tile([P, 1], F32, name="ones")
         nc.vector.memset(ones[:], 1.0)
         pos = const.tile([P, MT], F32, name="pos")
         nc.gpsimd.iota(pos[:], pattern=[[P, MT]], base=0, channel_multiplier=1,
                        allow_small_or_imprecise_dtypes=True)
+        ident = const.tile([P, P], F32, name="ident")
+        make_identity(nc, ident[:])
+        ident_b = const.tile([P, P], BF16, name="ident_b")
+        make_identity(nc, ident_b[:])
         turns = const.tile([P, NF], F32, name="turns")
         nc.vector.tensor_scalar(out=turns[:, 0:1], in0=ones[:], scalar1=1.0 / (2.0 * math.pi),
                                 scalar2=None, op0=ALU.mult)
@@ -172,6 +173,34 @@ def tile_groupedqueryattention_pa_kernel(tc, x, Wqkv, out_0, out_1, out_2):
                 if cut < nu:
                     nc.vector.tensor_copy(out=dst[:, cut:nu], in_=src[:, cut:nu])
 
+        staged = {}
+
+        def t_prep(i, h):
+            cg, g = divmod(i, PASSES)
+            wr = w_raw[(cg, g)]
+            if cg < 2:
+                src = wr[:].rearrange("p j (a y c) -> p y a c j", y=2, c=UNIT)[:, h]
+            elif h == 0:
+                src = None
+                srck = wr[:, :, 0:BANK].rearrange("p j (a y c) -> p y a c j", y=2, c=UNIT)
+            else:
+                src = wr[:, :, BANK:2 * BANK].rearrange("p j (a c) -> p a c j", c=UNIT)
+            staged[(i, h)] = []
+            for b in range(2):
+                st = psum.tile([P, 2 * BANK], BF16, name="bank")
+                staged[(i, h)].append(st)
+                for q in range(2):
+                    a0 = 8 * b + 4 * q
+                    rhs = src[:, a0:a0 + 4] if src is not None else srck[:, b, 4 * q:4 * q + 4]
+                    nc.tensor.matmul(out=st[:, q * BANK:(q + 1) * BANK].rearrange("p (a c j) -> p a c j", c=UNIT, j=PACK),
+                                     lhsT=ident_b[:], rhs=rhs, start=True, stop=True)
+
+        def s_evac(i, h):
+            wg = wstage.tile([P, BANK * PACK], BF16, name="wg", align_bytes=64)
+            w_grouped[(i, h)] = wg
+            for b in range(2):
+                nc.scalar.copy(out=wg[:, 2 * BANK * b:2 * BANK * (b + 1)], in_=staged[(i, h)][b][:])
+
         def w_quant(i, h):
             wq = wcodes.tile([P, BANK], U32, name="wq", align_bytes=64)
             ws = wcodes.tile([P, BANK], U8, name="ws", align_bytes=64)
@@ -241,7 +270,7 @@ def tile_groupedqueryattention_pa_kernel(tc, x, Wqkv, out_0, out_1, out_2):
                 in0=acc_rot.rearrange("p (h c) -> p h c", c=2 * NF),
                 in1=sin_t[:, m].rearrange("p s c -> p (s c)").unsqueeze(1).to_broadcast([P, nh, 2 * NF]),
                 op=ALU.mult)
-            if cg < 2:
+            if cg < 2 and m in (0, 3):
                 idle = psum.tile([P, BANK], F32, name="bank")
                 nc.tensor.matmul(out=idle[:], lhsT=ident[:], rhs=t1[:], start=True, stop=True)
             prods[(cg, m)] = (t1[:, 0:width].rearrange("p (h s c) -> p h s c", s=2, c=NF),
@@ -272,14 +301,17 @@ def tile_groupedqueryattention_pa_kernel(tc, x, Wqkv, out_0, out_1, out_2):
             quant_mm(i, 0)
             quant_mm(i, 1)
 
-        def q_epilogue(cg, fillers):
+        def q_epilogue(cg, fillers, tpiece):
             for m in range(MT):
                 plain_copy(cg, m)
                 rope_mults(cg, m)
+                if m == 1:
+                    t_prep(tpiece[0], tpiece[1])
                 if m >= 1:
                     rope_add_store(cg, m - 1)
             for (i, h) in fillers:
                 w_copy(i, h)
+            s_evac(tpiece[0], tpiece[1])
             rope_add_store(cg, MT - 1)
 
         copy2(0)
@@ -303,18 +335,17 @@ def tile_groupedqueryattention_pa_kernel(tc, x, Wqkv, out_0, out_1, out_2):
             copy2(i)
             quant_mm2(i)
         copy2(4)
-        q_epilogue(0, [(5, 0), (5, 1)])
+        q_epilogue(0, [(5, 0), (5, 1)], (6, 0))
         quant_mm2(4)
-        copy2(6)
+        w_copy(6, 1)
         quant_mm2(5)
         copy2(7)
         quant_mm2(6)
         w_copy(8, 0)
         quant_mm2(7)
         w_copy(9, 0)
-        q_epilogue(1, [(10, 0)])
+        q_epilogue(1, [(10, 0)], (11, 0))
         quant_mm(8, 0)
-        w_copy(11, 0)
         quant_mm(9, 0)
         w_copy(8, 1)
         quant_mm(10, 0)

@@ -63,12 +63,9 @@ def tile_groupedqueryattention_pa_kernel(tc, x, Wqkv, out_0, out_1, out_2):
             w_raw[(cg, g)] = wr
 
         load_w(0, 0)
-        load_x(0)
-        load_x(1)
-        load_w(0, 1)
-        load_x(2)
-        load_x(3)
-        for i in range(2, NCG * PASSES):
+        for m in range(MT):
+            load_x(m)
+        for i in range(1, NCG * PASSES):
             load_w(i // PASSES, i % PASSES)
 
         ones = const.tile([P, 1], F32, name="ones")
@@ -321,17 +318,13 @@ def tile_groupedqueryattention_pa_kernel(tc, x, Wqkv, out_0, out_1, out_2):
         x_quant(0)
         x_turn(1)
         x_quant(1)
-        copy2(1)
         x_turn(2)
-        w_quant(1, 0)
-        w_quant(1, 1)
         x_quant(2)
         x_turn(3)
         x_quant(3)
-        for i in range(2):
-            passes(i, 0)
-            passes(i, 1)
-        for i in range(2, 4):
+        passes(0, 0)
+        passes(0, 1)
+        for i in range(1, 4):
             copy2(i)
             quant_mm2(i)
         copy2(4)

@@ -135,12 +135,13 @@ def tile_groupedqueryattention_pa_kernel(tc, x, Wqkv, out_0, out_1, out_2):
             nc.vector.quantize_mx(out=xq[:, w0:w0 + PASSES * P].bitcast(FP8X4),
                                   scales=xs[:, w0:w0 + PASSES * P], in_=x_grouped[m][:])
 
-        SRC_RU = "p j (a y b i) -> p y a b i j"
-        SRC_V = "p j (a b i) -> p a b i j"
-        DST = "p (a b i j) -> p a b i j"
         NB = UNIT // 4
+        WALK = {"v": "i j", "s": "j i"}
 
-        def segments(cg, h, wr, wg):
+        def segments(cg, h, wr, wg, walk):
+            SRC_RU = "p j (a y b i) -> p y a b " + walk
+            SRC_V = "p j (a b i) -> p a b " + walk
+            DST = "p (a b i j) -> p a b " + walk
             if cg < 2:
                 return [(0, 16, wg[:].rearrange(DST, b=NB, i=4, j=PACK),
                          wr[:].rearrange(SRC_RU, y=2, b=NB, i=4)[:, h])]
@@ -160,12 +161,11 @@ def tile_groupedqueryattention_pa_kernel(tc, x, Wqkv, out_0, out_1, out_2):
             wg = wstage.tile([P, BANK * PACK], BF16, name="wg", align_bytes=64)
             w_grouped[(i, h)] = wg
             n_s = S_UNITS[cg][h]
-            segs = segments(cg, h, w_raw[(cg, g)], wg)
-            for (u0, nu, dst, src) in segs:
+            for (u0, nu, dst, src) in segments(cg, h, w_raw[(cg, g)], wg, WALK["s"]):
                 cut = min(max(n_s - u0, 0), nu)
                 if cut > 0:
                     nc.scalar.copy(out=dst[:, 0:cut], in_=src[:, 0:cut])
-            for (u0, nu, dst, src) in segs:
+            for (u0, nu, dst, src) in segments(cg, h, w_raw[(cg, g)], wg, WALK["v"]):
                 cut = min(max(n_s - u0, 0), nu)
                 if cut < nu:
                     nc.vector.tensor_copy(out=dst[:, cut:nu], in_=src[:, cut:nu])

@@ -28,7 +28,7 @@ NF = 32
 UNIT = 32
 UNITS = CG_COLS // UNIT
 
-S_UNITS = [[8, 6], [10, 10], [10, 12]]
+S_UNITS = [[8, 8], [10, 10], [10, 12]]
 
 
 def tile_groupedqueryattention_pa_kernel(tc, x, Wqkv, out_0, out_1, out_2):
@@ -42,7 +42,11 @@ def tile_groupedqueryattention_pa_kernel(tc, x, Wqkv, out_0, out_1, out_2):
         wcodes = ctx.enter_context(tc.tile_pool(name="wcodes", bufs=16))
         outp = ctx.enter_context(tc.tile_pool(name="outp", bufs=8))
         tmp = ctx.enter_context(tc.tile_pool(name="tmp", bufs=3))
-        psum = ctx.enter_context(tc.psum_pool(name="psum", bufs=8))
+        psum = ctx.enter_context(tc.psum_pool(name="psum", bufs=1))
+
+        def bank_of(cg, h, m):
+            return "bank%d" % ((4 + 2 * m + (h + cg) % 2) % 8)
+
         ctx.enter_context(tc.manual_schedule())
 
         x_raw = []
@@ -63,9 +67,14 @@ def tile_groupedqueryattention_pa_kernel(tc, x, Wqkv, out_0, out_1, out_2):
             w_raw[(cg, g)] = wr
 
         load_w(0, 0)
-        for m in range(MT):
-            load_x(m)
-        for i in range(1, NCG * PASSES):
+        load_x(0)
+        load_x(1)
+        load_w(0, 1)
+        load_w(0, 2)
+        load_w(0, 3)
+        load_x(2)
+        load_x(3)
+        for i in range(4, NCG * PASSES):
             load_w(i // PASSES, i % PASSES)
 
         ones = const.tile([P, 1], F32, name="ones")
@@ -120,7 +129,7 @@ def tile_groupedqueryattention_pa_kernel(tc, x, Wqkv, out_0, out_1, out_2):
             x_grouped[m] = xg
             xgw = xg[:].bitcast(F32)
             for b in range(2):
-                xt = psum.tile([P, BANK], F32, name="bank")
+                xt = psum.tile([P, BANK], F32, name="bank%d" % (2 * (m % 2) + b))
                 for gg in range(2):
                     g = 2 * b + gg
                     for u in range(2):
@@ -172,7 +181,7 @@ def tile_groupedqueryattention_pa_kernel(tc, x, Wqkv, out_0, out_1, out_2):
 
         staged = {}
 
-        def t_prep(i, h):
+        def t_prep(i, h, ms=(1, 2)):
             cg, g = divmod(i, PASSES)
             wr = w_raw[(cg, g)]
             if cg < 2:
@@ -184,7 +193,7 @@ def tile_groupedqueryattention_pa_kernel(tc, x, Wqkv, out_0, out_1, out_2):
                 src = wr[:, :, BANK:2 * BANK].rearrange("p j (a c) -> p a c j", c=UNIT)
             staged[(i, h)] = []
             for b in range(2):
-                st = psum.tile([P, 2 * BANK], BF16, name="bank")
+                st = psum.tile([P, 2 * BANK], BF16, name=bank_of(cg - 1 if g >= 2 else cg, 0, ms[b]))
                 staged[(i, h)].append(st)
                 for q in range(2):
                     a0 = 8 * b + 4 * q
@@ -206,13 +215,13 @@ def tile_groupedqueryattention_pa_kernel(tc, x, Wqkv, out_0, out_1, out_2):
 
         acc = {}
 
-        def passes(i, h):
+        def passes(i, h, ms=(0, 1, 2, 3)):
             cg, g = divmod(i, PASSES)
             wq, ws = w_codes[(i, h)]
-            for m in range(MT):
+            for m in ms:
                 w0 = (m * PASSES + g) * P
                 if g == 0:
-                    bank = psum.tile([P, BANK], F32, name="bank")
+                    bank = psum.tile([P, BANK], F32, name=bank_of(cg, h, m))
                     acc[(cg, h, m)] = bank
                 nc.tensor.matmul_mx(
                     out=acc[(cg, h, m)][:],
@@ -267,8 +276,8 @@ def tile_groupedqueryattention_pa_kernel(tc, x, Wqkv, out_0, out_1, out_2):
                 in0=acc_rot.rearrange("p (h c) -> p h c", c=2 * NF),
                 in1=sin_t[:, m].rearrange("p s c -> p (s c)").unsqueeze(1).to_broadcast([P, nh, 2 * NF]),
                 op=ALU.mult)
-            if cg < 2 and m in (0, 3):
-                idle = psum.tile([P, BANK], F32, name="bank")
+            if cg == 1 and m in (0, 3):
+                idle = psum.tile([P, BANK], F32, name=bank_of(cg, 0, m))
                 nc.tensor.matmul(out=idle[:], lhsT=ident[:], rhs=t1[:], start=True, stop=True)
             prods[(cg, m)] = (t1[:, 0:width].rearrange("p (h s c) -> p h s c", s=2, c=NF),
                               t2[:, 0:width].rearrange("p (h s c) -> p h s c", s=2, c=NF))
@@ -311,6 +320,7 @@ def tile_groupedqueryattention_pa_kernel(tc, x, Wqkv, out_0, out_1, out_2):
             s_evac(tpiece[0], tpiece[1])
             rope_add_store(cg, MT - 1)
 
+        LO, HI = (0, 1), (2, 3)
         copy2(0)
         x_turn(0)
         w_quant(0, 0)
@@ -318,18 +328,52 @@ def tile_groupedqueryattention_pa_kernel(tc, x, Wqkv, out_0, out_1, out_2):
         x_quant(0)
         x_turn(1)
         x_quant(1)
+        copy2(1)
+        passes(0, 0, LO)
+        passes(0, 1, LO)
+        for i in range(1, 3):
+            w_quant(i, 0)
+            w_quant(i, 1)
+            copy2(i + 1)
+            passes(i, 0, LO)
+            passes(i, 1, LO)
         x_turn(2)
-        x_quant(2)
         x_turn(3)
+        w_quant(3, 0)
+        w_quant(3, 1)
+        passes(3, 0, LO)
+        passes(3, 1, LO)
+        x_quant(2)
+        for i in range(4):
+            passes(i, 0, (2,))
+            passes(i, 1, (2,))
         x_quant(3)
-        passes(0, 0)
-        passes(0, 1)
-        for i in range(1, 4):
-            copy2(i)
-            quant_mm2(i)
+        for i in range(4):
+            passes(i, 0, (3,))
+            passes(i, 1, (3,))
+        plain_copy(0, 0)
+        rope_mults(0, 0)
+        plain_copy(0, 1)
+        rope_mults(0, 1)
+        rope_add_store(0, 0)
         copy2(4)
-        q_epilogue(0, [(5, 0), (5, 1)], (6, 0))
-        quant_mm2(4)
+        rope_add_store(0, 1)
+        w_quant(4, 0)
+        w_quant(4, 1)
+        passes(4, 0, LO)
+        passes(4, 1, LO)
+        w_copy(5, 0)
+        plain_copy(0, 2)
+        rope_mults(0, 2)
+        plain_copy(0, 3)
+        rope_mults(0, 3)
+        rope_add_store(0, 2)
+        passes(4, 0, HI)
+        t_prep(6, 0, HI)
+        w_copy(5, 1)
+        s_evac(6, 0)
+        passes(4, 1, HI)
+        rope_add_store(0, 3)
         w_copy(6, 1)
         quant_mm2(5)
         copy2(7)

@@ -276,7 +276,7 @@ def tile_groupedqueryattention_pa_kernel(tc, x, Wqkv, out_0, out_1, out_2):
                 in0=acc_rot.rearrange("p (h c) -> p h c", c=2 * NF),
                 in1=sin_t[:, m].rearrange("p s c -> p (s c)").unsqueeze(1).to_broadcast([P, nh, 2 * NF]),
                 op=ALU.mult)
-            if cg == 1 and m in (0, 3):
+            if cg == 1 and m == 0:
                 idle = psum.tile([P, BANK], F32, name=bank_of(cg, 0, m))
                 nc.tensor.matmul(out=idle[:], lhsT=ident[:], rhs=t1[:], start=True, stop=True)
             prods[(cg, m)] = (t1[:, 0:width].rearrange("p (h s c) -> p h s c", s=2, c=NF),
@@ -381,8 +381,21 @@ def tile_groupedqueryattention_pa_kernel(tc, x, Wqkv, out_0, out_1, out_2):
         w_copy(8, 0)
         quant_mm2(7)
         w_copy(9, 0)
-        q_epilogue(1, [(10, 0)], (11, 0))
-        quant_mm(8, 0)
+        for m in range(MT):
+            plain_copy(1, m)
+        rope_mults(1, 0)
+        rope_mults(1, 1)
+        t_prep(11, 0)
+        rope_add_store(1, 0)
+        w_quant(8, 0)
+        passes(8, 0)
+        rope_mults(1, 2)
+        rope_add_store(1, 1)
+        rope_mults(1, 3)
+        rope_add_store(1, 2)
+        w_copy(10, 0)
+        s_evac(11, 0)
+        rope_add_store(1, MT - 1)
         quant_mm(9, 0)
         w_copy(8, 1)
         quant_mm(10, 0)

from contextlib import ExitStack
import math

import concourse.mybir as mybir
from concourse.masks import make_identity

L, D, NOUT = 512, 2048, 3072
FLOPS = 2 * L * D * NOUT

F32 = mybir.dt.float32
BF16 = mybir.dt.bfloat16
U32 = mybir.dt.uint32
U8 = mybir.dt.uint8
I32 = mybir.dt.int32
FP8X4 = mybir.dt.float8_e5m2_x4
ALU = mybir.AluOpType
ACT = mybir.ActivationFunctionType

P = 128
PACK = 4
K_PASS = P * PACK
PASSES = D // K_PASS
MT = L // P
BANK = 512
CG_COLS = 1024
NCG = NOUT // CG_COLS
NF = 32
UNIT = 32
UNITS = CG_COLS // UNIT

S_UNITS = [[8, 8], [10, 10], [10, 12]]


def tile_groupedqueryattention_pa_kernel(tc, x, Wqkv, out_0, out_1, out_2):
    nc = tc.nc
    with ExitStack() as ctx:
        const = ctx.enter_context(tc.tile_pool(name="const", bufs=1))
        xin = ctx.enter_context(tc.tile_pool(name="xin", bufs=MT))
        xstage = ctx.enter_context(tc.tile_pool(name="xstage", bufs=2))
        win = ctx.enter_context(tc.tile_pool(name="win", bufs=8))
        wstage = ctx.enter_context(tc.tile_pool(name="wstage", bufs=8))
        wcodes = ctx.enter_context(tc.tile_pool(name="wcodes", bufs=16))
        outp = ctx.enter_context(tc.tile_pool(name="outp", bufs=8))
        tmp = ctx.enter_context(tc.tile_pool(name="tmp", bufs=3))
        psum = ctx.enter_context(tc.psum_pool(name="psum", bufs=1))

        def bank_of(cg, h, m):
            return "bank%d" % ((4 + 2 * m + (h + cg) % 2) % 8)

        ctx.enter_context(tc.manual_schedule())

        x_raw = []
        w_raw = {}

        def load_x(m):
            xr = xin.tile([P, D], BF16, name="xr")
            nc.sync.dma_start(out=xr[:], in_=x[m * P:(m + 1) * P, :])
            x_raw.append(xr)

        def load_w(cg, g):
            wr = win.tile([P, PACK, CG_COLS], BF16, name="wr")
            nc.sync.dma_start(
                out=wr[:],
                in_=Wqkv[g * K_PASS:(g + 1) * K_PASS, cg * CG_COLS:(cg + 1) * CG_COLS].rearrange(
                    "(p j) w -> p j w", j=PACK),
            )
            w_raw[(cg, g)] = wr

        load_w(0, 0)
        load_x(0)
        load_x(1)
        load_w(0, 1)
        load_w(0, 2)
        load_w(0, 3)
        load_x(2)
        load_x(3)
        for i in range(4, NCG * PASSES):
            load_w(i // PASSES, i % PASSES)

        ones = const.tile([P, 1], F32, name="ones")
        nc.vector.memset(ones[:], 1.0)
        pos = const.tile([P, MT], F32, name="pos")
        nc.gpsimd.iota(pos[:], pattern=[[P, MT]], base=0, channel_multiplier=1,
                       allow_small_or_imprecise_dtypes=True)
        ident = const.tile([P, P], F32, name="ident")
        make_identity(nc, ident[:])
        ident_b = const.tile([P, P], BF16, name="ident_b")
        make_identity(nc, ident_b[:])
        turns = const.tile([P, NF], F32, name="turns")
        nc.vector.tensor_scalar(out=turns[:, 0:1], in0=ones[:], scalar1=1.0 / (2.0 * math.pi),
                                scalar2=None, op0=ALU.mult)
        ratio = (1.0 / 1024.0) ** (1.0 / 31.0)
        for b in range(5):
            n = 2 ** b
            nc.vector.tensor_scalar(out=turns[:, n:2 * n], in0=turns[:, 0:n], scalar1=ratio ** n,
                                    scalar2=None, op0=ALU.mult)
        TW = MT * NF
        y = const.tile([P, MT, NF], F32, name="y")
        nc.vector.tensor_tensor(out=y[:], in0=pos[:].unsqueeze(2).to_broadcast([P, MT, NF]),
                                in1=turns[:].unsqueeze(1).to_broadcast([P, MT, NF]), op=ALU.mult)
        ki = const.tile([P, TW], I32, name="ki")
        yf = y[:].rearrange("p m f -> p (m f)")
        nc.vector.tensor_copy(out=ki[:], in_=yf)
        kf = const.tile([P, TW], F32, name="kf")
        nc.vector.tensor_copy(out=kf[:], in_=ki[:])
        fr = const.tile([P, TW], F32, name="fr")
        nc.vector.tensor_tensor(out=fr[:], in0=yf, in1=kf[:], op=ALU.subtract)
        wneg = const.tile([P, MT, NF], F32, name="wneg")
        wnf = wneg[:].rearrange("p m f -> p (m f)")
        nc.vector.scalar_tensor_tensor(out=wnf, in0=fr[:], scalar=0.5, in1=fr[:],
                                       op0=ALU.is_gt, op1=ALU.subtract)
        wabs = const.tile([P, MT, NF], F32, name="wabs")
        nc.vector.scalar_tensor_tensor(out=wabs[:].rearrange("p m f -> p (m f)"), in0=wnf, scalar=-1.0,
                                       in1=wnf, op0=ALU.mult, op1=ALU.max)
        sin_t = const.tile([P, MT, 2, NF], F32, name="sin_t")
        cos_t = const.tile([P, MT, NF], F32, name="cos_t")
        nc.scalar.activation(out=sin_t[:, :, 0, :], in_=wneg[:], func=ACT.Sin, scale=2.0 * math.pi)
        nc.scalar.activation(out=sin_t[:, :, 1, :], in_=wneg[:], func=ACT.Sin, scale=-2.0 * math.pi)
        nc.scalar.activation(out=cos_t[:], in_=wabs[:], func=ACT.Sin, scale=-2.0 * math.pi,
                             bias=math.pi / 2.0)

        xq = const.tile([P, MT * PASSES * P], U32, name="xq", align_bytes=64)
        xs = const.tile([P, MT * PASSES * P], U8, name="xs", align_bytes=64)
        x_grouped = {}

        def x_turn(m):
            words = x_raw[m][:].bitcast(F32)
            xg = xstage.tile([P, PASSES * P * PACK], BF16, name="xg", align_bytes=64)
            x_grouped[m] = xg
            xgw = xg[:].bitcast(F32)
            for b in range(2):
                xt = psum.tile([P, BANK], F32, name="bank%d" % (2 * (m % 2) + b))
                for gg in range(2):
                    g = 2 * b + gg
                    for u in range(2):
                        s = 2 * gg + u
                        nc.tensor.transpose(xt[:, s * P:(s + 1) * P],
                                            words[:, 256 * g + u:256 * (g + 1):2], ident[:])
                nc.scalar.copy(out=xgw[:, BANK * b:BANK * (b + 1)].rearrange("p (g r u) -> p g r u", g=2, u=2),
                               in_=xt[:].rearrange("p (g u r) -> p g r u", g=2, u=2))

        def x_quant(m):
            w0 = m * PASSES * P
            nc.vector.quantize_mx(out=xq[:, w0:w0 + PASSES * P].bitcast(FP8X4),
                                  scales=xs[:, w0:w0 + PASSES * P], in_=x_grouped[m][:])

        NB = UNIT // 4
        WALK = {"v": "i j", "s": "j i"}

        def segments(cg, h, wr, wg, walk):
            SRC_RU = "p j (a y b i) -> p y a b " + walk
            SRC_V = "p j (a b i) -> p a b " + walk
            DST = "p (a b i j) -> p a b " + walk
            if cg < 2:
                return [(0, 16, wg[:].rearrange(DST, b=NB, i=4, j=PACK),
                         wr[:].rearrange(SRC_RU, y=2, b=NB, i=4)[:, h])]
            if h == 0:
                srck = wr[:, :, 0:BANK].rearrange(SRC_RU, y=2, b=NB, i=4)
                half = BANK * PACK // 2
                return [(0, 8, wg[:, 0:half].rearrange(DST, b=NB, i=4, j=PACK), srck[:, 0]),
                        (8, 8, wg[:, half:2 * half].rearrange(DST, b=NB, i=4, j=PACK), srck[:, 1])]
            return [(0, 16, wg[:].rearrange(DST, b=NB, i=4, j=PACK),
                     wr[:, :, BANK:2 * BANK].rearrange(SRC_V, b=NB, i=4))]

        w_grouped = {}
        w_codes = {}

        def w_copy(i, h):
            cg, g = divmod(i, PASSES)
            wg = wstage.tile([P, BANK * PACK], BF16, name="wg", align_bytes=64)
            w_grouped[(i, h)] = wg
            n_s = S_UNITS[cg][h]
            for (u0, nu, dst, src) in segments(cg, h, w_raw[(cg, g)], wg, WALK["s"]):
                cut = min(max(n_s - u0, 0), nu)
                if cut > 0:
                    nc.scalar.copy(out=dst[:, 0:cut], in_=src[:, 0:cut])
            for (u0, nu, dst, src) in segments(cg, h, w_raw[(cg, g)], wg, WALK["v"]):
                cut = min(max(n_s - u0, 0), nu)
                if cut < nu:
                    nc.vector.tensor_copy(out=dst[:, cut:nu], in_=src[:, cut:nu])

        staged = {}

        def t_prep(i, h, ms=(1, 2)):
            cg, g = divmod(i, PASSES)
            wr = w_raw[(cg, g)]
            if cg < 2:
                src = wr[:].rearrange("p j (a y c) -> p y a c j", y=2, c=UNIT)[:, h]
            elif h == 0:
                src = None
                srck = wr[:, :, 0:BANK].rearrange("p j (a y c) -> p y a c j", y=2, c=UNIT)
            else:
                src = wr[:, :, BANK:2 * BANK].rearrange("p j (a c) -> p a c j", c=UNIT)
            staged[(i, h)] = []
            for b in range(2):
                st = psum.tile([P, 2 * BANK], BF16, name=bank_of(cg - 1 if g >= 2 else cg, 0, ms[b]))
                staged[(i, h)].append(st)
                for q in range(2):
                    a0 = 8 * b + 4 * q
                    rhs = src[:, a0:a0 + 4] if src is not None else srck[:, b, 4 * q:4 * q + 4]
                    nc.tensor.matmul(out=st[:, q * BANK:(q + 1) * BANK].rearrange("p (a c j) -> p a c j", c=UNIT, j=PACK),
                                     lhsT=ident_b[:], rhs=rhs, start=True, stop=True)

        def s_evac(i, h):
            wg = wstage.tile([P, BANK * PACK], BF16, name="wg", align_bytes=64)
            w_grouped[(i, h)] = wg
            for b in range(2):
                nc.scalar.copy(out=wg[:, 2 * BANK * b:2 * BANK * (b + 1)], in_=staged[(i, h)][b][:])

        def w_quant(i, h):
            wq = wcodes.tile([P, BANK], U32, name="wq", align_bytes=64)
            ws = wcodes.tile([P, BANK], U8, name="ws", align_bytes=64)
            nc.vector.quantize_mx(out=wq[:].bitcast(FP8X4), scales=ws[:], in_=w_grouped[(i, h)][:])
            w_codes[(i, h)] = (wq, ws)

        acc = {}

        def passes(i, h, ms=(0, 1, 2, 3)):
            cg, g = divmod(i, PASSES)
            wq, ws = w_codes[(i, h)]
            for m in ms:
                w0 = (m * PASSES + g) * P
                if g == 0:
                    bank = psum.tile([P, BANK], F32, name=bank_of(cg, h, m))
                    acc[(cg, h, m)] = bank
                nc.tensor.matmul_mx(
                    out=acc[(cg, h, m)][:],
                    lhsT=xq[:, w0:w0 + P].bitcast(FP8X4), lhsT_scale=xs[:, w0:w0 + P],
                    rhs=wq[:].bitcast(FP8X4), rhs_scale=ws[:],
                    start=(g == 0), stop=(g == PASSES - 1))

        out0v = out_0.rearrange("l h d -> l (h d)")
        out1v = out_1.rearrange("l h d -> l (h d)")
        out2v = out_2.rearrange("l h d -> l (h d)")
        prods = {}
        o_tiles = {}

        def o_tile(cg, m):
            if (cg, m) not in o_tiles:
                o = outp.tile([P, CG_COLS], F32, name="o")
                o_tiles[(cg, m)] = o
            return o_tiles[(cg, m)]

        def plain_copy(cg, m, eng_is_vector=False):
            o = o_tile(cg, m)
            if cg < 2:
                dst = o[:].rearrange("p (a y c) -> p y a c", y=2, c=NF)[:, 1]
                src = acc[(cg, 1, m)][:].rearrange("p (a c) -> p a c", c=NF)
            else:
                dst = o[:, BANK:2 * BANK]
                src = acc[(cg, 1, m)][:]
            if eng_is_vector:
                nc.vector.tensor_copy(out=dst, in_=src)
            else:
                nc.scalar.copy(out=dst, in_=src)
            if cg == 2:
                nc.sync.dma_start(out=out2v[m * P:(m + 1) * P, :], in_=o[:, BANK:2 * BANK])

        def k_plain_copy(m):
            o = o_tile(2, m)
            nc.scalar.copy(out=o[:, 0:BANK].rearrange("p (a y c) -> p y a c", y=2, c=NF)[:, 1],
                           in_=acc[(2, 0, m)][:, BANK // 2:BANK].rearrange("p (a c) -> p a c", c=NF))

        def rope_mults(cg, m):
            width = BANK if cg < 2 else BANK // 2
            nh = width // (2 * NF)
            acc_rot = acc[(cg, 0, m)][:, 0:width]
            t1 = tmp.tile([P, BANK], F32, name="t1")
            t2 = tmp.tile([P, BANK], F32, name="t2")
            nc.vector.tensor_tensor(
                out=t1[:, 0:width].rearrange("p (a c) -> p a c", c=NF),
                in0=acc_rot.rearrange("p (a c) -> p a c", c=NF),
                in1=cos_t[:, m, :].unsqueeze(1).to_broadcast([P, 2 * nh, NF]), op=ALU.mult)
            nc.vector.tensor_tensor(
                out=t2[:, 0:width].rearrange("p (h c) -> p h c", c=2 * NF),
                in0=acc_rot.rearrange("p (h c) -> p h c", c=2 * NF),
                in1=sin_t[:, m].rearrange("p s c -> p (s c)").unsqueeze(1).to_broadcast([P, nh, 2 * NF]),
                op=ALU.mult)
            if cg == 1 and m == 0:
                idle = psum.tile([P, BANK], F32, name=bank_of(cg, 0, m))
                nc.tensor.matmul(out=idle[:], lhsT=ident[:], rhs=t1[:], start=True, stop=True)
            prods[(cg, m)] = (t1[:, 0:width].rearrange("p (h s c) -> p h s c", s=2, c=NF),
                              t2[:, 0:width].rearrange("p (h s c) -> p h s c", s=2, c=NF))

        def rope_add_store(cg, m):
            t1v, t2v = prods[(cg, m)]
            o = o_tile(cg, m)
            rows = slice(m * P, (m + 1) * P)
            width = CG_COLS if cg < 2 else BANK
            o_rot = o[:, 0:width].rearrange("p (h s y c) -> p y h s c", s=2, y=2, c=NF)[:, 0]
            eng = nc.gpsimd
            eng.tensor_tensor(out=o_rot, in0=t1v, in1=t2v[:, :, ::-1, :], op=ALU.add)
            if cg < 2:
                nc.sync.dma_start(out=out0v[rows, cg * CG_COLS:(cg + 1) * CG_COLS], in_=o[:])
            else:
                nc.sync.dma_start(out=out1v[rows, :], in_=o[:, 0:BANK])

        def copy2(i):
            w_copy(i, 0)
            w_copy(i, 1)

        def quant_mm(i, h):
            w_quant(i, h)
            passes(i, h)

        def quant_mm2(i):
            quant_mm(i, 0)
            quant_mm(i, 1)

        def q_epilogue(cg, fillers, tpiece):
            for m in range(MT):
                plain_copy(cg, m)
                rope_mults(cg, m)
                if m == 1:
                    t_prep(tpiece[0], tpiece[1])
                if m >= 1:
                    rope_add_store(cg, m - 1)
            for (i, h) in fillers:
                w_copy(i, h)
            s_evac(tpiece[0], tpiece[1])
            rope_add_store(cg, MT - 1)

        LO, HI = (0, 1), (2, 3)
        copy2(0)
        x_turn(0)
        w_quant(0, 0)
        w_quant(0, 1)
        x_quant(0)
        x_turn(1)
        x_quant(1)
        copy2(1)
        passes(0, 0, LO)
        passes(0, 1, LO)
        for i in range(1, 3):
            w_quant(i, 0)
            w_quant(i, 1)
            copy2(i + 1)
            passes(i, 0, LO)
            passes(i, 1, LO)
        x_turn(2)
        x_turn(3)
        w_quant(3, 0)
        w_quant(3, 1)
        passes(3, 0, LO)
        passes(3, 1, LO)
        x_quant(2)
        for i in range(4):
            passes(i, 0, (2,))
            passes(i, 1, (2,))
        x_quant(3)
        for i in range(4):
            passes(i, 0, (3,))
            passes(i, 1, (3,))
        plain_copy(0, 0)
        rope_mults(0, 0)
        plain_copy(0, 1)
        rope_mults(0, 1)
        rope_add_store(0, 0)
        copy2(4)
        rope_add_store(0, 1)
        w_quant(4, 0)
        w_quant(4, 1)
        passes(4, 0, LO)
        passes(4, 1, LO)
        w_copy(5, 0)
        plain_copy(0, 2)
        rope_mults(0, 2)
        plain_copy(0, 3)
        rope_mults(0, 3)
        rope_add_store(0, 2)
        passes(4, 0, HI)
        t_prep(6, 0, HI)
        w_copy(5, 1)
        s_evac(6, 0)
        passes(4, 1, HI)
        rope_add_store(0, 3)
        w_copy(6, 1)
        quant_mm2(5)
        copy2(7)
        quant_mm2(6)
        w_copy(8, 0)
        quant_mm2(7)
        w_copy(9, 0)
        for m in range(MT):
            plain_copy(1, m)
        rope_mults(1, 0)
        rope_mults(1, 1)
        t_prep(11, 0)
        rope_add_store(1, 0)
        w_quant(8, 0)
        passes(8, 0)
        rope_mults(1, 2)
        rope_add_store(1, 1)
        rope_mults(1, 3)
        rope_add_store(1, 2)
        w_copy(10, 0)
        s_evac(11, 0)
        rope_add_store(1, MT - 1)
        quant_mm(9, 0)
        w_copy(8, 1)
        quant_mm(10, 0)
        w_copy(9, 1)
        quant_mm(11, 0)
        w_copy(10, 1)
        quant_mm(8, 1)
        rope_mults(2, 0)
        k_plain_copy(0)
        w_copy(11, 1)
        quant_mm(9, 1)
        rope_mults(2, 1)
        k_plain_copy(1)
        rope_add_store(2, 0)
        quant_mm(10, 1)
        rope_mults(2, 2)
        k_plain_copy(2)
        rope_add_store(2, 1)
        quant_mm(11, 1)
        rope_mults(2, 3)
        k_plain_copy(3)
        rope_add_store(2, 2)
        plain_copy(2, 0)
        plain_copy(2, 2, True)
        rope_add_store(2, 3)
        plain_copy(2, 1)
        plain_copy(2, 3, True)
